import numpy as np
import ml_dtypes


def mxq(x, axis, fmt="e4m3"):
    dtype, down = {"e4m3": (ml_dtypes.float8_e4m3fn, 7), "e5m2": (ml_dtypes.float8_e5m2, 14)}[fmt]
    v = np.moveaxis(np.asarray(x, np.float32).astype(ml_dtypes.bfloat16).astype(np.float64), axis, -1)
    blocks = v.reshape(v.shape[:-1] + (-1, 32))
    amax = np.abs(blocks).max(-1, keepdims=True)
    byte = np.maximum(np.where(amax > 0, np.frexp(amax)[1] - 1 + 127, 0) - down, 1)
    scale = np.exp2(byte - 127.0)
    codes = (blocks / scale).astype(np.float32).astype(dtype).astype(np.float64)
    return np.moveaxis((codes * scale).reshape(v.shape), -1, axis)


WIDE = False


def mx_kscale(k):
    if not WIDE:
        return np.ones(k)
    levels = np.array([10, -10, 5, -5, 0])
    a = np.random.permutation(np.resize(levels, k // 512 * 4)).reshape(k // 512, 4)
    idx = np.arange(k)
    return np.exp2(a[idx // 512, idx % 128 // 32])


BF16 = ml_dtypes.bfloat16


def bf(x):
    return np.asarray(x, np.float32).astype(BF16)


def f64(x):
    return np.asarray(x).astype(np.float64)


B, N, I, E = 2, 1024, 2048, 1024

EPS = 1e-07


def sigmoid(v):
    return 1.0 / (1.0 + np.exp(-v))


def setup_inputs():
    s = mx_kscale(E)
    c = np.sqrt(np.mean(s * s) * np.mean(1.0 / (s * s)))
    ru = np.exp(0.5 * np.random.standard_normal((B, N, 1)))
    ri = np.exp(0.5 * np.random.standard_normal((B, I, 1)))
    return {"user_emb": bf(np.random.standard_normal((B, N, E)) * ru * s),
            "item_emb": bf(np.random.standard_normal((B, I, E)) * ri / s),
            "proj_w": bf((1.5 + 0.1 * np.random.standard_normal((1, 1))) * np.sqrt(E) * c),
            "proj_b": bf(0.5 + 0.1 * np.random.standard_normal(1))}


def reference(user_emb, item_emb, proj_w, proj_b):
    user_emb, item_emb, proj_w, proj_b = f64(user_emb), f64(item_emb), f64(proj_w), f64(proj_b)
    u = user_emb / np.maximum(np.linalg.norm(user_emb, axis=-1, keepdims=True), EPS)
    v = item_emb / np.maximum(np.linalg.norm(item_emb, axis=-1, keepdims=True), EPS)
    cos_sim = mxq(v, 2, "e4m3") @ mxq(u, 2, "e4m3").transpose(0, 2, 1)
    return sigmoid(cos_sim * proj_w[0, 0] + proj_b[0])

@@ -1,0 +1,250 @@
+from contextlib import ExitStack
+
+import concourse.mybir as mybir
+from concourse.masks import make_identity
+
+F32 = mybir.dt.float32
+BF16 = mybir.dt.bfloat16
+U32 = mybir.dt.uint32
+U8 = mybir.dt.uint8
+FP8X4 = mybir.dt.float8_e4m3fn_x4
+ALU = mybir.AluOpType
+ACT = mybir.ActivationFunctionType
+
+P = 128
+B, N_USERS, N_ITEMS, E = 2, 1024, 2048, 1024
+UT = N_USERS // P
+IT = N_ITEMS // P
+EPS = 1e-07
+FLOPS = 2 * B * N_ITEMS * N_USERS * E
+
+PIN = True
+HEAD_SS = 28
+V_SS = (1, 3, 5, 7) + tuple(range(29, 46, 2))
+
+
+def tile_similarityoutputlayer_t_kernel(tc, user_emb, item_emb, proj_w, proj_b, out):
+    nc = tc.nc
+    with ExitStack() as ctx:
+        const = ctx.enter_context(tc.tile_pool(name="const", bufs=1))
+        xpool = ctx.enter_context(tc.tile_pool(name="x", bufs=1))
+        junk = ctx.enter_context(tc.tile_pool(name="junk", bufs=2))
+        small = ctx.enter_context(tc.tile_pool(name="small", bufs=3))
+        grp = ctx.enter_context(tc.tile_pool(name="grp", bufs=2))
+        codes = ctx.enter_context(tc.tile_pool(name="codes", bufs=1))
+        icodes = ctx.enter_context(tc.tile_pool(name="icodes", bufs=6))
+        opool = ctx.enter_context(tc.tile_pool(name="o", bufs=4))
+        ps_raw = ctx.enter_context(tc.psum_pool(name="ps_raw", bufs=4))
+        ps_rn = ctx.enter_context(tc.psum_pool(name="ps_rn", bufs=1))
+        ps_acc = ctx.enter_context(tc.psum_pool(name="ps_acc", bufs=3))
+        if PIN:
+            ctx.enter_context(tc.manual_schedule())
+
+        w_bf = const.tile([P, 1], BF16, name="w_bf")
+        b_bf = const.tile([P, 1], BF16, name="b_bf")
+        w_f = const.tile([P, 1], F32, name="w_f")
+        b_f = const.tile([P, 1], F32, name="b_f")
+        ident = const.tile([P, P], F32, name="ident")
+        neghalf = const.tile([P, 4], F32, name="neghalf")
+        ss = const.tile([P, 2 * (UT + IT), 8], F32, name="ss")
+        with nc.allow_non_contiguous_dma(reason="two scalars, one element to a partition"):
+            nc.scalar.dma_start(out=w_bf[:], in_=proj_w.rearrange("a b -> (a b)").partition_broadcast(P))
+            nc.scalar.dma_start(out=b_bf[:], in_=proj_b.partition_broadcast(P))
+        nc.gpsimd.memset(neghalf[:], -0.5)
+        make_identity(nc, ident[:])
+        warm = const.tile([P, 1], F32, name="warm")
+        nc.scalar.activation(out=warm[:], in_=neghalf[:, 0:1], func=ACT.Sigmoid)
+
+        xu = [xpool.tile([P, UT, E], BF16, name="xu%d" % b) for b in range(B)]
+        xi = [xpool.tile([P, IT, E], BF16, name="xi%d" % b) for b in range(B)]
+        for b in range(B):
+            src_u = user_emb[b].rearrange("(n p) k -> p n k", p=P)
+            cuts = (0, 1, 2, 3, 4, 5, 6, 7, 8) if b == 0 else (0, 2, 4, 8)
+            for lo, hi in zip(cuts[:-1], cuts[1:]):
+                nc.sync.dma_start(out=xu[b][:, lo:hi, :], in_=src_u[:, lo:hi, :])
+        for b in range(B):
+            src_i = item_emb[b].rearrange("(p m) k -> p m k", m=IT)
+            for lo in range(0, IT, 4):
+                nc.sync.dma_start(out=xi[b][:, lo : lo + 4, :], in_=src_i[:, lo : lo + 4, :])
+
+        tiles = []
+        for b in range(B):
+            tiles += [("U", b, n, xu[b][:, n, :]) for n in range(UT)]
+        for b in range(B):
+            tiles += [("I", b, m, xi[b][:, m, :]) for m in range(IT)]
+        n_tiles = len(tiles)
+
+        uc = [codes.tile([P, 2, N_USERS], U32, name="uc%d" % b, align_bytes=64) for b in range(B)]
+        us = [codes.tile([P, 2, N_USERS], U8, name="us%d" % b, align_bytes=64) for b in range(B)]
+
+        st = {}
+
+        def sum_squares(j):
+            x = tiles[j][3]
+            if j in V_SS:
+                stats = small.tile([P, 2, 6], F32, name="stats")
+                mv = small.tile([P, 2], F32, name="mv")
+                for c in range(2):
+                    nc.vector.bn_stats(out=stats[:, c, :], in_=x[:, c * 512 : (c + 1) * 512])
+                nc.vector.bn_aggr(out=mv[:], in_=stats[:].rearrange("p c s -> p (c s)"))
+                nc.vector.scalar_tensor_tensor(
+                    out=ss[:, j, 0:1], in0=mv[:, 0:1], scalar=mv[:, 0:1], in1=mv[:, 1:2], op0=ALU.mult, op1=ALU.add
+                )
+            else:
+                js = junk.tile([P, E], BF16, name="js")
+                nc.scalar.activation(out=js[:], in_=x, func=ACT.Square, scale=1.0 / 32.0, accum_out=ss[:, j, 0:1])
+
+        def recip_norm(g):
+            ssc = small.tile([P, 4], F32, name="ssc")
+            rn = small.tile([P, 4], F32, name="rn")
+            nc.gpsimd.tensor_scalar(
+                out=ssc[:], in0=ss[:, 4 * g : 4 * g + 4, 0], scalar1=float(E), scalar2=EPS * EPS, op0=ALU.mult, op1=ALU.max
+            )
+            nc.gpsimd.tensor_tensor(out=rn[:], in0=ssc[:], in1=neghalf[:], op=ALU.pow)
+            st["rn", g] = rn
+
+        def spread_norm(g):
+            rnp = ps_rn.tile([P, 4 * P], F32, name="rnp")
+            rn = st.pop(("rn", g))
+            for c in range(4):
+                nc.tensor.transpose(out=rnp[:, c * P : (c + 1) * P], in_=rn[:, c : c + 1].to_broadcast([P, P]), identity=ident[:])
+            st["rnp", g] = rnp
+
+        def copy_norm(g):
+            rnb = small.tile([P, 4 * P], F32, name="rnb")
+            nc.scalar.copy(out=rnb[:], in_=st.pop(("rnp", g))[:])
+            st["rnb", g] = rnb
+
+        def transposes(j):
+            xw = tiles[j][3].bitcast(F32)
+            raw = ps_raw.tile([P, 4 * P], F32, name="raw")
+            for u in range(2):
+                for g in range(2):
+                    nc.tensor.transpose(
+                        out=raw[:, (2 * u + g) * P : (2 * u + g + 1) * P],
+                        in_=xw[:, 256 * g + 128 * u : 256 * g + 128 * u + 128],
+                        identity=ident[:],
+                    )
+            st["raw", j] = raw
+
+        def scale(j):
+            kind, b, n, x = tiles[j]
+            raw = st.pop(("raw", j))
+            in0 = raw[:].bitcast(BF16).rearrange("p (u q e) -> p q u e", u=2, q=2 * P, e=2)
+            rnb = st["rnb", j // 4]
+            c = j % 4
+            in1 = rnb[:, c * P : (c + 1) * P].unsqueeze(1).unsqueeze(3).to_broadcast([P, 2, P, 4])
+            if kind == "U":
+                if c == 0:
+                    st["gq", j // 4] = grp.tile([P, 2, 4, P, 4], BF16, name="gq", align_bytes=64)
+                dst = st["gq", j // 4][:, :, c, :, :].rearrange("p g r t -> p g (r t)")
+            else:
+                gi = grp.tile([P, 2, P, 4], BF16, name="gi", bufs=4, align_bytes=64)
+                st["gi", j] = gi
+                dst = gi[:].rearrange("p g r t -> p (g r t)")
+            nc.vector.tensor_tensor(out=dst, in0=in0, in1=in1, op=ALU.mult)
+
+        def quantise(j):
+            kind, b, n, x = tiles[j]
+            if kind == "U":
+                if j % 4 != 3:
+                    return
+                gq = st.pop(("gq", j // 4))
+                h = n // 4
+                for g in range(2):
+                    nc.vector.quantize_mx(
+                        out=uc[b][:, g, h * 512 : (h + 1) * 512].bitcast(FP8X4),
+                        scales=us[b][:, g, h * 512 : (h + 1) * 512],
+                        in_=gq[:, g].rearrange("p n r t -> p (n r t)"),
+                    )
+            else:
+                gi = st.pop(("gi", j))
+                ic = icodes.tile([P, 2 * P], U32, name="ic", align_bytes=64)
+                isc = icodes.tile([P, 2 * P], U8, name="isc", align_bytes=64)
+                nc.vector.quantize_mx(out=ic[:].bitcast(FP8X4), scales=isc[:], in_=gi[:].rearrange("p g r t -> p (g r t)"))
+                st["ic", j] = (ic, isc)
+
+        def multiply(j):
+            kind, b, m, x = tiles[j]
+            if kind == "U":
+                return
+            ic, isc = st.pop(("ic", j))
+            for h in range(2):
+                acc = ps_acc.tile([P, 512], F32, name="acc")
+                for g in range(2):
+                    nc.tensor.matmul_mx(
+                        out=acc[:],
+                        lhsT=ic[:, g * P : (g + 1) * P].bitcast(FP8X4),
+                        lhsT_scale=isc[:, g * P : (g + 1) * P],
+                        rhs=uc[b][:, g, h * 512 : (h + 1) * 512].bitcast(FP8X4),
+                        rhs_scale=us[b][:, g, h * 512 : (h + 1) * 512],
+                        start=(g == 0),
+                        stop=(g == 1),
+                    )
+                st["acc", j, h] = acc
+
+        def sigmoid(j):
+            kind, b, m, x = tiles[j]
+            if kind == "U":
+                return
+            if m % 2 == 0:
+                st["o", b, m // 2] = opool.tile([P, 2, N_USERS], F32, name="o")
+            o = st["o", b, m // 2]
+            dst = out[b].rearrange("(p m) u -> p m u", m=IT)
+            for h in range(2):
+                acc = st.pop(("acc", j, h))
+                cols = slice(h * 512, (h + 1) * 512)
+                nc.scalar.activation(out=o[:, m % 2, cols], in_=acc[:], func=ACT.Sigmoid, bias=b_f[:, 0:1], scale=w_f[:, 0:1])
+                if j == n_tiles - 1:
+                    nc.sync.dma_start(out=dst[:, m, cols], in_=o[:, m % 2, cols])
+            if j == n_tiles - 2:
+                nc.sync.dma_start(out=dst[:, m, :], in_=o[:, m % 2, :])
+            elif m % 2 == 1 and j < n_tiles - 2:
+                nc.sync.dma_start(out=dst[:, m - 1 : m + 1, :], in_=o[:])
+
+        n_users = B * UT
+        ss_next = [0]
+        mm_next = [0]
+
+        def ss_upto(j_end):
+            while ss_next[0] < min(j_end, n_tiles):
+                sum_squares(ss_next[0])
+                ss_next[0] += 1
+
+        ss_upto(4)
+        recip_norm(0)
+        ss_upto(8)
+        spread_norm(0)
+        transposes(0)
+        transposes(1)
+        copy_norm(0)
+        recip_norm(1)
+        nc.vector.tensor_copy(out=w_f[:], in_=w_bf[:])
+        nc.vector.tensor_copy(out=b_f[:], in_=b_bf[:])
+        for i in range(n_tiles + 1):
+            if i < n_users:
+                ss_upto(8 + (i + 1) * (HEAD_SS - 8) // n_users)
+            else:
+                ss_upto(HEAD_SS + i - n_users + 1)
+            g_next = (i + 6) // 4
+            if (i + 6) % 4 == 0 and g_next * 4 < n_tiles and g_next >= 2:
+                ss_upto(4 * g_next + 4)
+                recip_norm(g_next)
+            if i % 2 == 0:
+                g_sp = (i + 4) // 4
+                if (i + 4) % 4 == 0 and g_sp * 4 < n_tiles:
+                    spread_norm(g_sp)
+                for j in (i + 2, i + 3):
+                    if j < n_tiles:
+                        transposes(j)
+            if (i + 3) % 4 == 0 and (i + 3) // 4 * 4 < n_tiles:
+                copy_norm((i + 3) // 4)
+            if i < n_tiles:
+                scale(i)
+            if 0 <= i - 1 < n_tiles:
+                quantise(i - 1)
+            if i % 2 == 0 or i >= n_tiles - 3:
+                while mm_next[0] < min(i, n_tiles):
+                    multiply(mm_next[0])
+                    sigmoid(mm_next[0])
+                    mm_next[0] += 1

@@ -18,9 +18,8 @@ IT = N_ITEMS // P
 EPS = 1e-07
 FLOPS = 2 * B * N_ITEMS * N_USERS * E
 
-PIN = True
-HEAD_SS = 28
-V_SS = (1, 3, 5, 7) + tuple(range(29, 46, 2))
+AHEAD = 6
+GRP = 2
 
 
 def tile_similarityoutputlayer_t_kernel(tc, user_emb, item_emb, proj_w, proj_b, out):
@@ -29,24 +28,26 @@ def tile_similarityoutputlayer_t_kernel(tc, user_emb, item_emb, proj_w, proj_b, 
         const = ctx.enter_context(tc.tile_pool(name="const", bufs=1))
         xpool = ctx.enter_context(tc.tile_pool(name="x", bufs=1))
         junk = ctx.enter_context(tc.tile_pool(name="junk", bufs=2))
-        small = ctx.enter_context(tc.tile_pool(name="small", bufs=3))
-        grp = ctx.enter_context(tc.tile_pool(name="grp", bufs=2))
+        xspool = ctx.enter_context(tc.tile_pool(name="xs", bufs=4))
+        grp = ctx.enter_context(tc.tile_pool(name="grp", bufs=4))
         codes = ctx.enter_context(tc.tile_pool(name="codes", bufs=1))
-        icodes = ctx.enter_context(tc.tile_pool(name="icodes", bufs=6))
+        icodes = ctx.enter_context(tc.tile_pool(name="icodes", bufs=4))
         opool = ctx.enter_context(tc.tile_pool(name="o", bufs=4))
         ps_raw = ctx.enter_context(tc.psum_pool(name="ps_raw", bufs=4))
-        ps_rn = ctx.enter_context(tc.psum_pool(name="ps_rn", bufs=1))
-        ps_acc = ctx.enter_context(tc.psum_pool(name="ps_acc", bufs=3))
-        if PIN:
-            ctx.enter_context(tc.manual_schedule())
+        ps_acc = ctx.enter_context(tc.psum_pool(name="ps_acc", bufs=4))
+        ctx.enter_context(tc.manual_schedule())
+
+        n_tiles = B * (UT + IT)
 
         w_bf = const.tile([P, 1], BF16, name="w_bf")
         b_bf = const.tile([P, 1], BF16, name="b_bf")
         w_f = const.tile([P, 1], F32, name="w_f")
         b_f = const.tile([P, 1], F32, name="b_f")
         ident = const.tile([P, P], F32, name="ident")
-        neghalf = const.tile([P, 4], F32, name="neghalf")
-        ss = const.tile([P, 2 * (UT + IT), 8], F32, name="ss")
+        neghalf = const.tile([P, GRP], F32, name="neghalf")
+        ssq = const.tile([P, n_tiles, 8], F32, name="ssq")
+        ssc = const.tile([P, n_tiles], F32, name="ssc")
+        rn = const.tile([P, n_tiles], F32, name="rn")
         with nc.allow_non_contiguous_dma(reason="two scalars, one element to a partition"):
             nc.scalar.dma_start(out=w_bf[:], in_=proj_w.rearrange("a b -> (a b)").partition_broadcast(P))
             nc.scalar.dma_start(out=b_bf[:], in_=proj_b.partition_broadcast(P))
@@ -72,51 +73,40 @@ def tile_similarityoutputlayer_t_kernel(tc, user_emb, item_emb, proj_w, proj_b, 
             tiles += [("U", b, n, xu[b][:, n, :]) for n in range(UT)]
         for b in range(B):
             tiles += [("I", b, m, xi[b][:, m, :]) for m in range(IT)]
-        n_tiles = len(tiles)
 
         uc = [codes.tile([P, 2, N_USERS], U32, name="uc%d" % b, align_bytes=64) for b in range(B)]
         us = [codes.tile([P, 2, N_USERS], U8, name="us%d" % b, align_bytes=64) for b in range(B)]
 
         st = {}
 
-        def sum_squares(j):
+        def is_item(j):
+            return 0 <= j < n_tiles and tiles[j][0] == "I"
+
+        def sum_squares(j, on_vector):
             x = tiles[j][3]
-            if j in V_SS:
-                stats = small.tile([P, 2, 6], F32, name="stats")
-                mv = small.tile([P, 2], F32, name="mv")
-                for c in range(2):
-                    nc.vector.bn_stats(out=stats[:, c, :], in_=x[:, c * 512 : (c + 1) * 512])
-                nc.vector.bn_aggr(out=mv[:], in_=stats[:].rearrange("p c s -> p (c s)"))
+            if on_vector:
+                jv = junk.tile([P, E], F32, name="jv")
                 nc.vector.scalar_tensor_tensor(
-                    out=ss[:, j, 0:1], in0=mv[:, 0:1], scalar=mv[:, 0:1], in1=mv[:, 1:2], op0=ALU.mult, op1=ALU.add
+                    out=jv[:], in0=x, scalar=1.0, in1=x, op0=ALU.mult, op1=ALU.mult, accum_out=ssq[:, j, 0:1]
                 )
             else:
                 js = junk.tile([P, E], BF16, name="js")
-                nc.scalar.activation(out=js[:], in_=x, func=ACT.Square, scale=1.0 / 32.0, accum_out=ss[:, j, 0:1])
+                nc.scalar.activation(out=js[:], in_=x, func=ACT.Square, accum_out=ssq[:, j, 0:1])
 
         def recip_norm(g):
-            ssc = small.tile([P, 4], F32, name="ssc")
-            rn = small.tile([P, 4], F32, name="rn")
+            cols = slice(GRP * g, GRP * g + GRP)
             nc.gpsimd.tensor_scalar(
-                out=ssc[:], in0=ss[:, 4 * g : 4 * g + 4, 0], scalar1=float(E), scalar2=EPS * EPS, op0=ALU.mult, op1=ALU.max
+                out=ssc[:, cols], in0=ssq[:, cols, 0], scalar1=1.0, scalar2=EPS * EPS, op0=ALU.mult, op1=ALU.max
             )
-            nc.gpsimd.tensor_tensor(out=rn[:], in0=ssc[:], in1=neghalf[:], op=ALU.pow)
-            st["rn", g] = rn
+            nc.gpsimd.tensor_tensor(out=rn[:, cols], in0=ssc[:, cols], in1=neghalf[:], op=ALU.pow)
 
-        def spread_norm(g):
-            rnp = ps_rn.tile([P, 4 * P], F32, name="rnp")
-            rn = st.pop(("rn", g))
-            for c in range(4):
-                nc.tensor.transpose(out=rnp[:, c * P : (c + 1) * P], in_=rn[:, c : c + 1].to_broadcast([P, P]), identity=ident[:])
-            st["rnp", g] = rnp
-
-        def copy_norm(g):
-            rnb = small.tile([P, 4 * P], F32, name="rnb")
-            nc.scalar.copy(out=rnb[:], in_=st.pop(("rnp", g))[:])
-            st["rnb", g] = rnb
+        def scale(j):
+            xs = xspool.tile([P, E], BF16, name="xs")
+            nc.vector.tensor_scalar(out=xs[:], in0=tiles[j][3], scalar1=rn[:, j : j + 1], scalar2=None, op0=ALU.mult)
+            st["xs", j] = xs
 
         def transposes(j):
-            xw = tiles[j][3].bitcast(F32)
+            xw = st.pop(("xs", j))[:].bitcast(F32)
             raw = ps_raw.tile([P, 4 * P], F32, name="raw")
             for u in range(2):
                 for g in range(2):
@@ -127,38 +117,29 @@ def tile_similarityoutputlayer_t_kernel(tc, user_emb, item_emb, proj_w, proj_b, 
                     )
             st["raw", j] = raw
 
-        def scale(j):
-            kind, b, n, x = tiles[j]
+        def copy_out(j, on_vector):
             raw = st.pop(("raw", j))
-            in0 = raw[:].bitcast(BF16).rearrange("p (u q e) -> p q u e", u=2, q=2 * P, e=2)
-            rnb = st["rnb", j // 4]
-            c = j % 4
-            in1 = rnb[:, c * P : (c + 1) * P].unsqueeze(1).unsqueeze(3).to_broadcast([P, 2, P, 4])
-            if kind == "U":
-                if c == 0:
-                    st["gq", j // 4] = grp.tile([P, 2, 4, P, 4], BF16, name="gq", align_bytes=64)
-                dst = st["gq", j // 4][:, :, c, :, :].rearrange("p g r t -> p g (r t)")
+            gi = grp.tile([P, 2, P, 4], BF16, name="gi", align_bytes=64)
+            dst = gi[:].rearrange("p g r t -> p (g r t)").bitcast(F32).rearrange("p (q u) -> p q u", u=2)
+            src = raw[:].rearrange("p (u q) -> p q u", u=2)
+            if on_vector:
+                nc.vector.tensor_copy(out=dst, in_=src)
             else:
-                gi = grp.tile([P, 2, P, 4], BF16, name="gi", bufs=4, align_bytes=64)
-                st["gi", j] = gi
-                dst = gi[:].rearrange("p g r t -> p (g r t)")
-            nc.vector.tensor_tensor(out=dst, in0=in0, in1=in1, op=ALU.mult)
+                nc.scalar.copy(out=dst, in_=src)
+            st["gi", j] = gi
 
         def quantise(j):
             kind, b, n, x = tiles[j]
+            gi = st.pop(("gi", j))
             if kind == "U":
-                if j % 4 != 3:
-                    return
-                gq = st.pop(("gq", j // 4))
-                h = n // 4
+                cols = slice(n * P, (n + 1) * P)
                 for g in range(2):
                     nc.vector.quantize_mx(
-                        out=uc[b][:, g, h * 512 : (h + 1) * 512].bitcast(FP8X4),
-                        scales=us[b][:, g, h * 512 : (h + 1) * 512],
-                        in_=gq[:, g].rearrange("p n r t -> p (n r t)"),
+                        out=uc[b][:, g, cols].bitcast(FP8X4),
+                        scales=us[b][:, g, cols],
+                        in_=gi[:, g].rearrange("p r t -> p (r t)"),
                     )
             else:
-                gi = st.pop(("gi", j))
                 ic = icodes.tile([P, 2 * P], U32, name="ic", align_bytes=64)
                 isc = icodes.tile([P, 2 * P], U8, name="isc", align_bytes=64)
                 nc.vector.quantize_mx(out=ic[:].bitcast(FP8X4), scales=isc[:], in_=gi[:].rearrange("p g r t -> p (g r t)"))
@@ -166,8 +147,6 @@ def tile_similarityoutputlayer_t_kernel(tc, user_emb, item_emb, proj_w, proj_b, 
 
         def multiply(j):
             kind, b, m, x = tiles[j]
-            if kind == "U":
-                return
             ic, isc = st.pop(("ic", j))
             for h in range(2):
                 acc = ps_acc.tile([P, 512], F32, name="acc")
@@ -185,8 +164,6 @@ def tile_similarityoutputlayer_t_kernel(tc, user_emb, item_emb, proj_w, proj_b, 
 
         def sigmoid(j):
             kind, b, m, x = tiles[j]
-            if kind == "U":
-                return
             if m % 2 == 0:
                 st["o", b, m // 2] = opool.tile([P, 2, N_USERS], F32, name="o")
             o = st["o", b, m // 2]
@@ -202,49 +179,45 @@ def tile_similarityoutputlayer_t_kernel(tc, user_emb, item_emb, proj_w, proj_b, 
             elif m % 2 == 1 and j < n_tiles - 2:
                 nc.sync.dma_start(out=dst[:, m - 1 : m + 1, :], in_=o[:])
 
-        n_users = B * UT
         ss_next = [0]
         mm_next = [0]
+        sg_next = [0]
 
-        def ss_upto(j_end):
-            while ss_next[0] < min(j_end, n_tiles):
-                sum_squares(ss_next[0])
-                ss_next[0] += 1
+        def next_ss(on_vector):
+            j = ss_next[0]
+            sum_squares(j, on_vector)
+            ss_next[0] += 1
+            if j % GRP == GRP - 1:
+                recip_norm(j // GRP)
 
-        ss_upto(4)
-        recip_norm(0)
-        ss_upto(8)
-        spread_norm(0)
-        transposes(0)
-        transposes(1)
-        copy_norm(0)
-        recip_norm(1)
+        for k in range(AHEAD):
+            next_ss(k % 2 == 1)
         nc.vector.tensor_copy(out=w_f[:], in_=w_bf[:])
         nc.vector.tensor_copy(out=b_f[:], in_=b_bf[:])
-        for i in range(n_tiles + 1):
-            if i < n_users:
-                ss_upto(8 + (i + 1) * (HEAD_SS - 8) // n_users)
-            else:
-                ss_upto(HEAD_SS + i - n_users + 1)
-            g_next = (i + 6) // 4
-            if (i + 6) % 4 == 0 and g_next * 4 < n_tiles and g_next >= 2:
-                ss_upto(4 * g_next + 4)
-                recip_norm(g_next)
+        for i in range(-4, n_tiles + 6):
+            tail = i >= n_tiles - 1
+            if 0 <= i < n_tiles:
+                quantise(i)
+            has_sig = False
+            while sg_next[0] < mm_next[0] and (sg_next[0] <= i - 3 or tail):
+                if is_item(sg_next[0]):
+                    sigmoid(sg_next[0])
+                    has_sig = True
+                sg_next[0] += 1
             if i % 2 == 0:
-                g_sp = (i + 4) // 4
-                if (i + 4) % 4 == 0 and g_sp * 4 < n_tiles:
-                    spread_norm(g_sp)
                 for j in (i + 2, i + 3):
-                    if j < n_tiles:
+                    if 0 <= j < n_tiles:
                         transposes(j)
-            if (i + 3) % 4 == 0 and (i + 3) // 4 * 4 < n_tiles:
-                copy_norm((i + 3) // 4)
-            if i < n_tiles:
-                scale(i)
-            if 0 <= i - 1 < n_tiles:
-                quantise(i - 1)
-            if i % 2 == 0 or i >= n_tiles - 3:
+            if i % 2 == 0 or tail:
                 while mm_next[0] < min(i, n_tiles):
-                    multiply(mm_next[0])
-                    sigmoid(mm_next[0])
+                    if is_item(mm_next[0]):
+                        multiply(mm_next[0])
                     mm_next[0] += 1
+            more = ss_next[0] < n_tiles
+            v_ss = more and has_sig
+            if 0 <= i + 1 < n_tiles:
+                copy_out(i + 1, not v_ss)
+            if 0 <= i + 4 < n_tiles:
+                scale(i + 4)
+            if more and ss_next[0] <= i + 4 + AHEAD:
+                next_ss(v_ss)

@@ -85,7 +85,7 @@ def tile_similarityoutputlayer_t_kernel(tc, user_emb, item_emb, proj_w, proj_b, 
         def sum_squares(j, on_vector):
             x = tiles[j][3]
             if on_vector:
-                jv = junk.tile([P, E], F32, name="jv")
+                jv = junk.tile([P, E], BF16, name="jv")
                 nc.vector.scalar_tensor_tensor(
                     out=jv[:], in0=x, scalar=1.0, in1=x, op0=ALU.mult, op1=ALU.mult, accum_out=ssq[:, j, 0:1]
                 )

@@ -35,7 +35,7 @@ def tile_similarityoutputlayer_t_kernel(tc, user_emb, item_emb, proj_w, proj_b, 
         opool = ctx.enter_context(tc.tile_pool(name="o", bufs=4))
         ps_raw = ctx.enter_context(tc.psum_pool(name="ps_raw", bufs=4))
         ps_acc = ctx.enter_context(tc.psum_pool(name="ps_acc", bufs=4))
-        ctx.enter_context(tc.manual_schedule())
+        ctx.enter_context(tc.manual_schedule(engines={mybir.EngineType.PE, mybir.EngineType.SP}))
 
         n_tiles = B * (UT + IT)
 

from contextlib import ExitStack

import concourse.mybir as mybir
from concourse.masks import make_identity

F32 = mybir.dt.float32
BF16 = mybir.dt.bfloat16
U32 = mybir.dt.uint32
U8 = mybir.dt.uint8
FP8X4 = mybir.dt.float8_e4m3fn_x4
ALU = mybir.AluOpType
ACT = mybir.ActivationFunctionType

P = 128
B, N_USERS, N_ITEMS, E = 2, 1024, 2048, 1024
UT = N_USERS // P
IT = N_ITEMS // P
EPS = 1e-07
FLOPS = 2 * B * N_ITEMS * N_USERS * E

AHEAD = 6
GRP = 2


def tile_similarityoutputlayer_t_kernel(tc, user_emb, item_emb, proj_w, proj_b, out):
    nc = tc.nc
    with ExitStack() as ctx:
        const = ctx.enter_context(tc.tile_pool(name="const", bufs=1))
        xpool = ctx.enter_context(tc.tile_pool(name="x", bufs=1))
        junk = ctx.enter_context(tc.tile_pool(name="junk", bufs=2))
        xspool = ctx.enter_context(tc.tile_pool(name="xs", bufs=4))
        grp = ctx.enter_context(tc.tile_pool(name="grp", bufs=4))
        codes = ctx.enter_context(tc.tile_pool(name="codes", bufs=1))
        icodes = ctx.enter_context(tc.tile_pool(name="icodes", bufs=4))
        opool = ctx.enter_context(tc.tile_pool(name="o", bufs=4))
        ps_raw = ctx.enter_context(tc.psum_pool(name="ps_raw", bufs=4))
        ps_acc = ctx.enter_context(tc.psum_pool(name="ps_acc", bufs=4))
        ctx.enter_context(tc.manual_schedule(engines={mybir.EngineType.PE, mybir.EngineType.SP}))

        n_tiles = B * (UT + IT)

        w_bf = const.tile([P, 1], BF16, name="w_bf")
        b_bf = const.tile([P, 1], BF16, name="b_bf")
        w_f = const.tile([P, 1], F32, name="w_f")
        b_f = const.tile([P, 1], F32, name="b_f")
        ident = const.tile([P, P], F32, name="ident")
        neghalf = const.tile([P, GRP], F32, name="neghalf")
        ssq = const.tile([P, n_tiles, 8], F32, name="ssq")
        ssc = const.tile([P, n_tiles], F32, name="ssc")
        rn = const.tile([P, n_tiles], F32, name="rn")
        with nc.allow_non_contiguous_dma(reason="two scalars, one element to a partition"):
            nc.scalar.dma_start(out=w_bf[:], in_=proj_w.rearrange("a b -> (a b)").partition_broadcast(P))
            nc.scalar.dma_start(out=b_bf[:], in_=proj_b.partition_broadcast(P))
        nc.gpsimd.memset(neghalf[:], -0.5)
        make_identity(nc, ident[:])
        warm = const.tile([P, 1], F32, name="warm")
        nc.scalar.activation(out=warm[:], in_=neghalf[:, 0:1], func=ACT.Sigmoid)

        xu = [xpool.tile([P, UT, E], BF16, name="xu%d" % b) for b in range(B)]
        xi = [xpool.tile([P, IT, E], BF16, name="xi%d" % b) for b in range(B)]
        for b in range(B):
            src_u = user_emb[b].rearrange("(n p) k -> p n k", p=P)
            cuts = (0, 1, 2, 3, 4, 5, 6, 7, 8) if b == 0 else (0, 2, 4, 8)
            for lo, hi in zip(cuts[:-1], cuts[1:]):
                nc.sync.dma_start(out=xu[b][:, lo:hi, :], in_=src_u[:, lo:hi, :])
        for b in range(B):
            src_i = item_emb[b].rearrange("(p m) k -> p m k", m=IT)
            for lo in range(0, IT, 4):
                nc.sync.dma_start(out=xi[b][:, lo : lo + 4, :], in_=src_i[:, lo : lo + 4, :])

        tiles = []
        for b in range(B):
            tiles += [("U", b, n, xu[b][:, n, :]) for n in range(UT)]
        for b in range(B):
            tiles += [("I", b, m, xi[b][:, m, :]) for m in range(IT)]

        uc = [codes.tile([P, 2, N_USERS], U32, name="uc%d" % b, align_bytes=64) for b in range(B)]
        us = [codes.tile([P, 2, N_USERS], U8, name="us%d" % b, align_bytes=64) for b in range(B)]

        st = {}

        def is_item(j):
            return 0 <= j < n_tiles and tiles[j][0] == "I"

        def sum_squares(j, on_vector):
            x = tiles[j][3]
            if on_vector:
                jv = junk.tile([P, E], BF16, name="jv")
                nc.vector.scalar_tensor_tensor(
                    out=jv[:], in0=x, scalar=1.0, in1=x, op0=ALU.mult, op1=ALU.mult, accum_out=ssq[:, j, 0:1]
                )
            else:
                js = junk.tile([P, E], BF16, name="js")
                nc.scalar.activation(out=js[:], in_=x, func=ACT.Square, accum_out=ssq[:, j, 0:1])

        def recip_norm(g):
            cols = slice(GRP * g, GRP * g + GRP)
            nc.gpsimd.tensor_scalar(
                out=ssc[:, cols], in0=ssq[:, cols, 0], scalar1=1.0, scalar2=EPS * EPS, op0=ALU.mult, op1=ALU.max
            )
            nc.gpsimd.tensor_tensor(out=rn[:, cols], in0=ssc[:, cols], in1=neghalf[:], op=ALU.pow)

        def scale(j):
            xs = xspool.tile([P, E], BF16, name="xs")
            nc.vector.tensor_scalar(out=xs[:], in0=tiles[j][3], scalar1=rn[:, j : j + 1], scalar2=None, op0=ALU.mult)
            st["xs", j] = xs

        def transposes(j):
            xw = st.pop(("xs", j))[:].bitcast(F32)
            raw = ps_raw.tile([P, 4 * P], F32, name="raw")
            for u in range(2):
                for g in range(2):
                    nc.tensor.transpose(
                        out=raw[:, (2 * u + g) * P : (2 * u + g + 1) * P],
                        in_=xw[:, 256 * g + 128 * u : 256 * g + 128 * u + 128],
                        identity=ident[:],
                    )
            st["raw", j] = raw

        def copy_out(j, on_vector):
            raw = st.pop(("raw", j))
            gi = grp.tile([P, 2, P, 4], BF16, name="gi", align_bytes=64)
            dst = gi[:].rearrange("p g r t -> p (g r t)").bitcast(F32).rearrange("p (q u) -> p q u", u=2)
            src = raw[:].rearrange("p (u q) -> p q u", u=2)
            if on_vector:
                nc.vector.tensor_copy(out=dst, in_=src)
            else:
                nc.scalar.copy(out=dst, in_=src)
            st["gi", j] = gi

        def quantise(j):
            kind, b, n, x = tiles[j]
            gi = st.pop(("gi", j))
            if kind == "U":
                cols = slice(n * P, (n + 1) * P)
                for g in range(2):
                    nc.vector.quantize_mx(
                        out=uc[b][:, g, cols].bitcast(FP8X4),
                        scales=us[b][:, g, cols],
                        in_=gi[:, g].rearrange("p r t -> p (r t)"),
                    )
            else:
                ic = icodes.tile([P, 2 * P], U32, name="ic", align_bytes=64)
                isc = icodes.tile([P, 2 * P], U8, name="isc", align_bytes=64)
                nc.vector.quantize_mx(out=ic[:].bitcast(FP8X4), scales=isc[:], in_=gi[:].rearrange("p g r t -> p (g r t)"))
                st["ic", j] = (ic, isc)

        def multiply(j):
            kind, b, m, x = tiles[j]
            ic, isc = st.pop(("ic", j))
            for h in range(2):
                acc = ps_acc.tile([P, 512], F32, name="acc")
                for g in range(2):
                    nc.tensor.matmul_mx(
                        out=acc[:],
                        lhsT=ic[:, g * P : (g + 1) * P].bitcast(FP8X4),
                        lhsT_scale=isc[:, g * P : (g + 1) * P],
                        rhs=uc[b][:, g, h * 512 : (h + 1) * 512].bitcast(FP8X4),
                        rhs_scale=us[b][:, g, h * 512 : (h + 1) * 512],
                        start=(g == 0),
                        stop=(g == 1),
                    )
                st["acc", j, h] = acc

        def sigmoid(j):
            kind, b, m, x = tiles[j]
            if m % 2 == 0:
                st["o", b, m // 2] = opool.tile([P, 2, N_USERS], F32, name="o")
            o = st["o", b, m // 2]
            dst = out[b].rearrange("(p m) u -> p m u", m=IT)
            for h in range(2):
                acc = st.pop(("acc", j, h))
                cols = slice(h * 512, (h + 1) * 512)
                nc.scalar.activation(out=o[:, m % 2, cols], in_=acc[:], func=ACT.Sigmoid, bias=b_f[:, 0:1], scale=w_f[:, 0:1])
                if j == n_tiles - 1:
                    nc.sync.dma_start(out=dst[:, m, cols], in_=o[:, m % 2, cols])
            if j == n_tiles - 2:
                nc.sync.dma_start(out=dst[:, m, :], in_=o[:, m % 2, :])
            elif m % 2 == 1 and j < n_tiles - 2:
                nc.sync.dma_start(out=dst[:, m - 1 : m + 1, :], in_=o[:])

        ss_next = [0]
        mm_next = [0]
        sg_next = [0]

        def next_ss(on_vector):
            j = ss_next[0]
            sum_squares(j, on_vector)
            ss_next[0] += 1
            if j % GRP == GRP - 1:
                recip_norm(j // GRP)

        for k in range(AHEAD):
            next_ss(k % 2 == 1)
        nc.vector.tensor_copy(out=w_f[:], in_=w_bf[:])
        nc.vector.tensor_copy(out=b_f[:], in_=b_bf[:])
        for i in range(-4, n_tiles + 6):
            tail = i >= n_tiles - 1
            if 0 <= i < n_tiles:
                quantise(i)
            has_sig = False
            while sg_next[0] < mm_next[0] and (sg_next[0] <= i - 3 or tail):
                if is_item(sg_next[0]):
                    sigmoid(sg_next[0])
                    has_sig = True
                sg_next[0] += 1
            if i % 2 == 0:
                for j in (i + 2, i + 3):
                    if 0 <= j < n_tiles:
                        transposes(j)
            if i % 2 == 0 or tail:
                while mm_next[0] < min(i, n_tiles):
                    if is_item(mm_next[0]):
                        multiply(mm_next[0])
                    mm_next[0] += 1
            more = ss_next[0] < n_tiles
            v_ss = more and has_sig
            if 0 <= i + 1 < n_tiles:
                copy_out(i + 1, not v_ss)
            if 0 <= i + 4 < n_tiles:
                scale(i + 4)
            if more and ss_next[0] <= i + 4 + AHEAD:
                next_ss(v_ss)
